import numpy as np
import ml_dtypes


BF16 = ml_dtypes.bfloat16


def bf(x):
    return np.asarray(x, np.float32).astype(BF16)


def f64(x):
    return np.asarray(x).astype(np.float64)


E2M1 = np.array([0.0, 0.5, 1.0, 1.5, 2.0, 3.0, 4.0, 6.0, -0.0, -0.5, -1.0, -1.5, -2.0, -3.0, -4.0, -6.0])


def pack_weight(w, fmt):
    k, n = w.shape
    w = f64(bf(w)).reshape(k // 32, 32, n)
    amax = np.abs(w).max(1)
    if fmt == "e4m3":
        byte = np.frexp(amax)[1] - 1 + 127 - 7
    else:
        mant, ex = np.frexp(amax / 6.0)
        byte = np.where(mant > 0.5, ex, ex - 1) + 127
    byte = np.clip(np.where(amax > 0, byte, 1), 1, 254)
    scaled = (w * np.exp2(127.0 - byte)[:, None, :]).reshape(k, n).astype(np.float32)
    by_word = np.ascontiguousarray(scaled.reshape(k // 512, 128, 4, n).transpose(0, 1, 3, 2))
    if fmt == "e4m3":
        words = by_word.astype(ml_dtypes.float8_e4m3fn).view(np.uint8)
    else:
        c = by_word.astype(ml_dtypes.float4_e2m1fn).view(np.uint8) & 0xF
        words = c[..., 0::2] | (c[..., 1::2] << 4)
    return np.ascontiguousarray(words), np.ascontiguousarray(byte.astype(np.uint8).reshape(k // 512, 16, n))


def unpack_weight(words, scales, fmt):
    g, p, n, _ = words.shape
    if fmt == "e4m3":
        vals = np.ascontiguousarray(words).view(ml_dtypes.float8_e4m3fn).astype(np.float64)
    else:
        nib = np.empty((g, p, n, 4), np.uint8)
        nib[..., 0::2] = words & 0xF
        nib[..., 1::2] = words >> 4
        vals = E2M1[nib]
    vals = vals * np.repeat(np.exp2(scales.astype(np.float64) - 127.0), 8, axis=1)[..., None]
    return vals.transpose(0, 1, 3, 2).reshape(g * 512, n)

def pack4(w):
    words, scales = pack_weight(w, "e2m1")
    return words.reshape(words.shape[0], 128, -1), scales


def unpack4(words, scales):
    return unpack_weight(words.reshape(words.shape[0], 128, -1, 2), scales, "e2m1")


def kspread(k):
    return np.exp2(np.repeat(np.random.randint(-6, 7, k // 32), 32).astype(np.float64))


B, D, H = 512, 2048, 4096
M_SCALE = 1.5


def setup_inputs():
    s, t = kspread(D), kspread(H)
    x = np.random.standard_normal((B, D)) * s
    h_prev = np.random.standard_normal((B, H)) * t
    c_prev = bf(np.random.standard_normal((B, H)))
    W_ih = np.random.standard_normal((2 * H, D)) * 0.7 / np.sqrt(D) / s[None, :]
    b_ih = bf(np.random.standard_normal(2 * H) * 0.2)
    W_hh = np.random.standard_normal((2 * H, H)) * 0.7 / np.sqrt(H) / t[None, :]
    b_hh = bf(np.random.standard_normal(2 * H) * 0.2)
    log_lambda = bf(np.log(np.random.uniform(0.05, 0.5, H)))
    z_bias = bf(np.random.standard_normal(H) * 0.2)
    m_bias = bf(np.random.standard_normal(H) * 0.2)
    x_words, x_scales = pack4(np.ascontiguousarray(x.T))
    h_prev_words, h_prev_scales = pack4(np.ascontiguousarray(h_prev.T))
    W_ih_words, W_ih_scales = pack4(np.ascontiguousarray(W_ih.T))
    W_hh_words, W_hh_scales = pack4(np.ascontiguousarray(W_hh.T))
    return {'x_words': x_words,
            'x_scales': x_scales,
            'h_prev_words': h_prev_words,
            'h_prev_scales': h_prev_scales,
            'c_prev': c_prev,
            'W_ih_words': W_ih_words,
            'W_ih_scales': W_ih_scales,
            'b_ih': b_ih,
            'W_hh_words': W_hh_words,
            'W_hh_scales': W_hh_scales,
            'b_hh': b_hh,
            'log_lambda': log_lambda,
            'z_bias': z_bias,
            'm_bias': m_bias}


def reference(x_words, x_scales, h_prev_words, h_prev_scales, c_prev, W_ih_words, W_ih_scales, b_ih, W_hh_words, W_hh_scales, b_hh, log_lambda, z_bias, m_bias):
    gates = ((unpack4(x_words, x_scales).T @ unpack4(W_ih_words, W_ih_scales)) + f64(b_ih)
             + (unpack4(h_prev_words, h_prev_scales).T @ unpack4(W_hh_words, W_hh_scales)) + f64(b_hh))
    z_raw, m_raw = gates[:, :H], gates[:, H:]
    z_t = np.tanh(z_raw + f64(z_bias))
    M_t = M_SCALE * np.tanh(m_raw + f64(m_bias))
    A_base = -np.exp(f64(log_lambda))
    innov = z_t - M_t * (A_base * f64(c_prev))
    return z_t, M_t, innov

@@ -1,0 +1,275 @@
+from contextlib import ExitStack
+
+import concourse.mybir as mybir
+from concourse.masks import make_identity
+
+F32 = mybir.dt.float32
+BF16 = mybir.dt.bfloat16
+I32 = mybir.dt.int32
+U8 = mybir.dt.uint8
+FP4X4 = mybir.dt.float4_e2m1fn_x4
+ACT = mybir.ActivationFunctionType
+ALU = mybir.AluOpType
+
+B, D, H = 512, 2048, 4096
+M_SCALE = 1.5
+FLOPS = 2 * B * (D + H) * 2 * H
+
+P = 128
+X_PASSES = D // 512
+H_PASSES = H // 512
+PASSES = X_PASSES + H_PASSES
+T_TILES = B // P
+N = 512
+PAIRS = H // N
+BLOCKS = PAIRS // 2
+OUTER = 8
+
+
+def tile_koslmcell_pa_kernel(
+    tc, x_words, x_scales, h_words, h_scales, c_prev, wih_words, wih_scales, b_ih,
+    whh_words, whh_scales, b_hh, log_lambda, z_bias, m_bias, out_z, out_m, out_innov,
+):
+    nc = tc.nc
+
+    with ExitStack() as ctx:
+        keep = ctx.enter_context(tc.tile_pool(name="keep", bufs=1))
+        wpool = ctx.enter_context(tc.tile_pool(name="wpool", bufs=4 * PASSES))
+        work = ctx.enter_context(tc.tile_pool(name="work", bufs=3))
+        psum = ctx.enter_context(tc.psum_pool(name="psum", bufs=1))
+
+        act = keep.tile([P, PASSES, 2 * B], U8, name="act", align_bytes=256)
+        act_sc = keep.tile([P, PASSES, B], U8, name="act_sc", align_bytes=256)
+        planes = []
+        for i in range(4):
+            planes.append(keep.tile([P, PASSES * 2 * N], U8, name="plane%d" % i, align_bytes=256))
+        ident = keep.tile([P, P], BF16, name="ident")
+        rows = keep.tile([P, 7, 32], BF16, name="rows")
+        rows4 = keep.tile([P, 7 * P], BF16, name="rows4")
+        cols = keep.tile([P, 7 * P], F32, name="cols")
+        bias_cols = keep.tile([P, 2 * P], F32, name="bias_cols")
+        exp_cols = keep.tile([P, P], F32, name="exp_cols")
+
+        def plane(block, pair, half):
+            if block == 0:
+                region = planes[pair][:, half * PASSES * N : (half + 1) * PASSES * N]
+                return region.rearrange("p (g n) -> p g n", n=N)
+            whole = planes[2 * (block % 2) + half][:].rearrange("p (g n) -> p g n", n=2 * N)
+            return whole[:, :, pair * N : (pair + 1) * N]
+
+        def scale_rows(dst, src, c0, width, g0, g1, first):
+            for quad in (0, 2, 1, 3):
+                nc.sync.dma_start(
+                    out=dst[32 * quad : 32 * quad + 4, g0 + first : g1 + first, :].bitcast(I32),
+                    in_=src[g0:g1, 4 * quad : 4 * quad + 4, c0 : c0 + width].rearrange("g q n -> q g n").bitcast(I32),
+                )
+
+        def words_of(g):
+            return wih_words[g] if g < X_PASSES else whh_words[g - X_PASSES]
+
+        w_tiles = {}
+
+        def load_first_codes(pair, g):
+            w = wpool.tile([P, 4 * N], U8, name="w", align_bytes=256)
+            src = words_of(g).rearrange("p (h n) -> p h n", h=2)[:, :, 2 * N * pair : 2 * N * (pair + 1)]
+            nc.sync.dma_start(
+                out=w[:].rearrange("p (h n) -> p h n", h=2).bitcast(I32),
+                in_=src.bitcast(I32),
+            )
+            w_tiles[(0, pair, g)] = w
+
+        def load_codes(block, half, g):
+            w = wpool.tile([P, 4 * N], U8, name="w", align_bytes=256)
+            c0 = 2 * H * half + 4 * N * block
+            nc.sync.dma_start(out=w[:].bitcast(I32), in_=words_of(g)[:, c0 : c0 + 4 * N].bitcast(I32))
+            w_tiles[(block, half, g)] = w
+
+        def load_block(block):
+            for half in (1, 0):
+                dst = planes[2 * (block % 2) + half][:].rearrange("p (g n) -> p g n", n=2 * N)
+                c0 = H * half + 2 * N * block
+                scale_rows(dst, wih_scales, c0, 2 * N, 0, X_PASSES, 0)
+                scale_rows(dst, whh_scales, c0, 2 * N, 0, H_PASSES, X_PASSES)
+                for g in range(PASSES):
+                    load_codes(block, half, g)
+
+        def codes(block, pair, half, g):
+            if block == 0:
+                return w_tiles[(0, pair, g)][:, 2 * N * half : 2 * N * (half + 1)]
+            return w_tiles[(block, half, g)][:, 2 * N * pair : 2 * N * (pair + 1)]
+
+        def matmul(acc, j, t, half, g, n0=0, n1=N):
+            block, pair = j // 2, j % 2
+            nc.tensor.matmul_mx(
+                out=acc[:, 0 : n1 - n0],
+                lhsT=act[:, g, 2 * P * t : 2 * P * (t + 1)].bitcast(FP4X4),
+                lhsT_scale=act_sc[:, g, P * t : P * (t + 1)],
+                rhs=codes(block, pair, half, g)[:, 2 * n0 : 2 * n1].bitcast(FP4X4),
+                rhs_scale=plane(block, pair, half)[:, g, n0:n1],
+                start=(g == 0),
+                stop=(g == PASSES - 1),
+            )
+
+        def bank(i):
+            return psum.tile([P, N], F32, name="bank%d" % i)
+
+        c_view = c_prev.rearrange("(t p) n -> p t n", p=P)
+        c_tiles = {}
+
+        def load_c(j):
+            c = work.tile([P, T_TILES, N], BF16, name="c", bufs=2)
+            nc.gpsimd.dma_start(out=c[:], in_=c_view[:, :, j * N : (j + 1) * N])
+            c_tiles[j] = c
+
+        spread = {}
+
+        def spread_columns(j):
+            for key, src in (
+                ("m", bias_cols[:, P + 16 * j : P + 16 * j + 16]),
+                ("z", bias_cols[:, 16 * j : 16 * j + 16]),
+                ("e", exp_cols[:, 16 * j : 16 * j + 16]),
+            ):
+                wide = work.tile([P, N], F32, name="wide", bufs=2, align_bytes=64)
+                nc.scalar.copy(
+                    out=wide[:].rearrange("p (b i) -> p b i", i=32),
+                    in_=src.unsqueeze(2).to_broadcast([P, 16, 32]),
+                )
+                full = work.tile([P, N], F32, name="full_" + key, bufs=2, align_bytes=64)
+                nc.vector.transpose(full[:], wide[:])
+                spread[(key, j)] = full
+
+        def store(j, out, t, n0, n1, tile):
+            eng = nc.sync if j >= PAIRS - 2 else nc.gpsimd
+            eng.dma_start(out=out[P * t : P * (t + 1), j * N + n0 : j * N + n1], in_=tile)
+
+        prods = {}
+
+        def finish_m(j, t, acc):
+            a = work.tile([P, N], F32, name="a")
+            nc.vector.tensor_tensor(out=a[:], in0=acc[:], in1=spread[("m", j)][:], op=ALU.add)
+            nc.scalar.activation(out=a[:], in_=a[:], func=ACT.Tanh)
+            big_m = work.tile([P, N], F32, name="big_m")
+            nc.scalar.mul(out=big_m[:], in_=a[:], mul=M_SCALE)
+            store(j, out_m, t, 0, N, big_m[:])
+            prod = work.tile([P, N], F32, name="prod", bufs=4)
+            nc.vector.tensor_tensor(out=prod[:], in0=c_tiles[j][:, t, :], in1=spread[("e", j)][:], op=ALU.mult)
+            nc.vector.tensor_tensor(out=prod[:], in0=prod[:], in1=big_m[:], op=ALU.mult)
+            prods[(j, t)] = prod
+
+        def finish_z(j, t, acc, n0=0, n1=N):
+            w = n1 - n0
+            z = work.tile([P, N], F32, name="z")
+            nc.vector.tensor_tensor(out=z[:, 0:w], in0=acc[:, 0:w], in1=spread[("z", j)][:, n0:n1], op=ALU.add)
+            nc.scalar.activation(out=z[:, 0:w], in_=z[:, 0:w], func=ACT.Tanh)
+            store(j, out_z, t, n0, n1, z[:, 0:w])
+            innov = prods[(j, t)][:, n0:n1]
+            nc.vector.tensor_tensor(out=innov, in0=innov, in1=z[:, 0:w], op=ALU.add)
+            store(j, out_innov, t, n0, n1, innov)
+
+        def zero(view):
+            nc.vector.memset(view.bitcast(I32), 0)
+
+        with tc.manual_schedule():
+            nc.gpsimd.dma_start(out=rows[:, 0:2, :], in_=b_ih.rearrange("(s b k) -> b s k", s=2, k=32))
+            nc.gpsimd.dma_start(out=rows[:, 2:4, :], in_=b_hh.rearrange("(s b k) -> b s k", s=2, k=32))
+            nc.gpsimd.dma_start(out=rows[:, 4, :], in_=z_bias.rearrange("(b k) -> b k", k=32))
+            nc.gpsimd.dma_start(out=rows[:, 5, :], in_=m_bias.rearrange("(b k) -> b k", k=32))
+            nc.gpsimd.dma_start(out=rows[:, 6, :], in_=log_lambda.rearrange("(b k) -> b k", k=32))
+            make_identity(nc, ident[:])
+            load_c(0)
+
+            z0, m0 = plane(0, 0, 0), plane(0, 0, 1)
+            zero(act_sc[:, 0:X_PASSES, :])
+            zero(z0[:, 0:X_PASSES, :])
+            zero(m0[:, 0:X_PASSES, :])
+            zero(act_sc[:, X_PASSES:PASSES, :])
+            zero(z0[:, X_PASSES:PASSES, :])
+            zero(m0[:, X_PASSES:PASSES, :])
+            nc.vector.tensor_copy(
+                out=rows4[:].rearrange("p (s a k) -> p s a k", s=7, a=4),
+                in_=rows[:].unsqueeze(2).to_broadcast([P, 7, 4, 32]),
+            )
+            zero(planes[1][:])
+            zero(planes[3][:])
+            zero(planes[2][:])
+
+            nc.sync.dma_start(out=act[:, 0, :].bitcast(I32), in_=x_words[0].bitcast(I32))
+            load_first_codes(0, 0)
+            scale_rows(act_sc, x_scales, 0, B, 0, X_PASSES, 0)
+            scale_rows(z0, wih_scales, 0, N, 0, X_PASSES, 0)
+            scale_rows(m0, wih_scales, H, N, 0, X_PASSES, 0)
+            nc.sync.dma_start(
+                out=act[:, 1:X_PASSES, :].bitcast(I32),
+                in_=x_words[1:X_PASSES].rearrange("g p n -> p g n").bitcast(I32),
+            )
+            for g in range(1, X_PASSES):
+                load_first_codes(0, g)
+            scale_rows(act_sc, h_scales, 0, B, 0, H_PASSES, X_PASSES)
+            scale_rows(z0, whh_scales, 0, N, 0, H_PASSES, X_PASSES)
+            scale_rows(m0, whh_scales, H, N, 0, H_PASSES, X_PASSES)
+            for part in range(2):
+                nc.sync.dma_start(
+                    out=act[:, X_PASSES + 4 * part : X_PASSES + 4 * part + 4, :].bitcast(I32),
+                    in_=h_words[4 * part : 4 * part + 4].rearrange("g p n -> p g n").bitcast(I32),
+                )
+                for g in range(X_PASSES + 4 * part, X_PASSES + 4 * part + 4):
+                    load_first_codes(0, g)
+            for half in (1, 0):
+                dst = plane(0, 1, half)
+                scale_rows(dst, wih_scales, H * half + N, N, 0, X_PASSES, 0)
+                scale_rows(dst, whh_scales, H * half + N, N, 0, H_PASSES, X_PASSES)
+            for g in range(PASSES):
+                load_first_codes(1, g)
+            load_block(1)
+
+            turned = psum.tile([P, 2 * N], BF16, name="bank7")
+            acc = {}
+            order = [(0, t) for t in range(T_TILES)] + [(1, t) for t in range(T_TILES)]
+            for i, (half, t) in enumerate(order[:-1]):
+                acc[(half, t)] = bank(i)
+            for g in range(2):
+                for half, t in order[:-1]:
+                    matmul(acc[(half, t)], 0, t, half, g)
+            for s in range(7):
+                nc.tensor.transpose(turned[:, P * s : P * (s + 1)], rows4[:, P * s : P * (s + 1)], ident[:])
+            nc.scalar.copy(out=cols[:], in_=turned[:, 0 : 7 * P])
+            nc.vector.tensor_tensor(
+                out=bias_cols[:], in0=cols[:, 0 : 2 * P], in1=cols[:, 2 * P : 4 * P], op=ALU.add
+            )
+            nc.vector.tensor_tensor(out=bias_cols[:], in0=bias_cols[:], in1=cols[:, 4 * P : 6 * P], op=ALU.add)
+            nc.scalar.activation(out=exp_cols[:], in_=cols[:, 6 * P : 7 * P], func=ACT.Exp)
+            spread_columns(0)
+            acc[(1, 3)] = bank(7)
+            for g in range(2):
+                matmul(acc[(1, 3)], 0, 3, 1, g)
+            for g in range(2, OUTER):
+                for half, t in order:
+                    matmul(acc[(half, t)], 0, t, half, g)
+            load_c(1)
+            for t in range(T_TILES):
+                for half in (1, 0):
+                    for g in range(OUTER, PASSES):
+                        matmul(acc[(half, t)], 0, t, half, g)
+                finish_m(0, t, acc[(1, t)])
+                finish_z(0, t, acc[(0, t)])
+            spread_columns(1)
+
+            for j in range(1, PAIRS):
+                if j % 2 == 0 and j // 2 + 1 < BLOCKS:
+                    load_block(j // 2 + 1)
+                if j + 1 < PAIRS:
+                    load_c(j + 1)
+                for t in range(T_TILES):
+                    last = j == PAIRS - 1 and t == T_TILES - 1
+                    m_acc = bank(4 + t)
+                    for g in range(PASSES):
+                        matmul(m_acc, j, t, 1, g)
+                    finish_m(j, t, m_acc)
+                    edges = [0, 256, 384, 512] if last else [0, N]
+                    for i in range(len(edges) - 1):
+                        z_acc = bank((t + i) % T_TILES)
+                        for g in range(PASSES):
+                            matmul(z_acc, j, t, 0, g, edges[i], edges[i + 1])
+                        finish_z(j, t, z_acc, edges[i], edges[i + 1])
+                    if t == 1 and j + 1 < PAIRS:
+                        spread_columns(j + 1)

@@ -64,6 +64,18 @@ def tile_koslmcell_pa_kernel(
                     in_=src[g0:g1, 4 * quad : 4 * quad + 4, c0 : c0 + width].rearrange("g q n -> q g n").bitcast(I32),
                 )
 
+        def scale_row(dst, src, c0, width, first, r):
+            nc.sync.dma_start(
+                out=dst[r:P:32, first : first + src.shape[0], :].bitcast(I32),
+                in_=src[:, r:16:4, c0 : c0 + width].rearrange("g q n -> q g n").bitcast(I32),
+            )
+
+        def load_act(src, first, g0, g1):
+            nc.sync.dma_start(
+                out=act[:, first + g0 : first + g1, :].bitcast(I32),
+                in_=src[g0:g1].rearrange("g p n -> p g n").bitcast(I32),
+            )
+
         def words_of(g):
             return wih_words[g] if g < X_PASSES else whh_words[g - X_PASSES]
 
@@ -85,13 +97,15 @@ def tile_koslmcell_pa_kernel(
             w_tiles[(block, half, g)] = w
 
         def load_block(block):
-            for half in (1, 0):
-                dst = planes[2 * (block % 2) + half][:].rearrange("p (g n) -> p g n", n=2 * N)
-                c0 = H * half + 2 * N * block
-                scale_rows(dst, wih_scales, c0, 2 * N, 0, X_PASSES, 0)
-                scale_rows(dst, whh_scales, c0, 2 * N, 0, H_PASSES, X_PASSES)
-                for g in range(PASSES):
-                    load_codes(block, half, g)
+            for r in range(4):
+                for half in (1, 0):
+                    dst = planes[2 * (block % 2) + half][:].rearrange("p (g n) -> p g n", n=2 * N)
+                    c0 = H * half + 2 * N * block
+                    scale_row(dst, wih_scales, c0, 2 * N, 0, r)
+                    scale_row(dst, whh_scales, c0, 2 * N, X_PASSES, r)
+                for half in (1, 0):
+                    for g in range(3 * r, 3 * r + 3):
+                        load_codes(block, half, g)
 
         def codes(block, pair, half, g):
             if block == 0:
@@ -156,12 +170,19 @@ def tile_koslmcell_pa_kernel(
             nc.vector.tensor_tensor(out=prod[:], in0=prod[:], in1=big_m[:], op=ALU.mult)
             prods[(j, t)] = prod
 
-        def finish_z(j, t, acc, n0=0, n1=N):
+        zs = {}
+
+        def start_z(j, t, acc, n0=0, n1=N):
             w = n1 - n0
             z = work.tile([P, N], F32, name="z")
             nc.vector.tensor_tensor(out=z[:, 0:w], in0=acc[:, 0:w], in1=spread[("z", j)][:, n0:n1], op=ALU.add)
             nc.scalar.activation(out=z[:, 0:w], in_=z[:, 0:w], func=ACT.Tanh)
             store(j, out_z, t, n0, n1, z[:, 0:w])
+            zs[(j, t, n0)] = z
+
+        def end_z(j, t, n0=0, n1=N):
+            w = n1 - n0
+            z = zs[(j, t, n0)]
             innov = prods[(j, t)][:, n0:n1]
             nc.vector.tensor_tensor(out=innov, in0=innov, in1=z[:, 0:w], op=ALU.add)
             store(j, out_innov, t, n0, n1, innov)
@@ -170,6 +191,8 @@ def tile_koslmcell_pa_kernel(
             nc.vector.memset(view.bitcast(I32), 0)
 
         with tc.manual_schedule():
+            zeros = keep.tile([P, N], BF16, name="zeros")
+            nc.gpsimd.memset(zeros[:], 0.0)
             nc.gpsimd.dma_start(out=rows[:, 0:2, :], in_=b_ih.rearrange("(s b k) -> b s k", s=2, k=32))
             nc.gpsimd.dma_start(out=rows[:, 2:4, :], in_=b_hh.rearrange("(s b k) -> b s k", s=2, k=32))
             nc.gpsimd.dma_start(out=rows[:, 4, :], in_=z_bias.rearrange("(b k) -> b k", k=32))
@@ -177,6 +200,10 @@ def tile_koslmcell_pa_kernel(
             nc.gpsimd.dma_start(out=rows[:, 6, :], in_=log_lambda.rearrange("(b k) -> b k", k=32))
             make_identity(nc, ident[:])
             load_c(0)
+
+            warm = bank(7)
+            for i in range(7):
+                nc.tensor.matmul(warm[:], lhsT=zeros[:, 0:P], rhs=zeros[:], start=True, stop=True)
 
             z0, m0 = plane(0, 0, 0), plane(0, 0, 1)
             zero(act_sc[:, 0:X_PASSES, :])
@@ -193,33 +220,30 @@ def tile_koslmcell_pa_kernel(
             zero(planes[3][:])
             zero(planes[2][:])
 
-            nc.sync.dma_start(out=act[:, 0, :].bitcast(I32), in_=x_words[0].bitcast(I32))
+            load_act(x_words, 0, 0, 1)
             load_first_codes(0, 0)
             scale_rows(act_sc, x_scales, 0, B, 0, X_PASSES, 0)
             scale_rows(z0, wih_scales, 0, N, 0, X_PASSES, 0)
             scale_rows(m0, wih_scales, H, N, 0, X_PASSES, 0)
-            nc.sync.dma_start(
-                out=act[:, 1:X_PASSES, :].bitcast(I32),
-                in_=x_words[1:X_PASSES].rearrange("g p n -> p g n").bitcast(I32),
-            )
+            load_act(x_words, 0, 1, 4)
             for g in range(1, X_PASSES):
                 load_first_codes(0, g)
             scale_rows(act_sc, h_scales, 0, B, 0, H_PASSES, X_PASSES)
             scale_rows(z0, whh_scales, 0, N, 0, H_PASSES, X_PASSES)
+            load_act(h_words, X_PASSES, 0, 4)
+            load_first_codes(0, X_PASSES)
             scale_rows(m0, whh_scales, H, N, 0, H_PASSES, X_PASSES)
-            for part in range(2):
-                nc.sync.dma_start(
-                    out=act[:, X_PASSES + 4 * part : X_PASSES + 4 * part + 4, :].bitcast(I32),
-                    in_=h_words[4 * part : 4 * part + 4].rearrange("g p n -> p g n").bitcast(I32),
-                )
-                for g in range(X_PASSES + 4 * part, X_PASSES + 4 * part + 4):
-                    load_first_codes(0, g)
-            for half in (1, 0):
-                dst = plane(0, 1, half)
-                scale_rows(dst, wih_scales, H * half + N, N, 0, X_PASSES, 0)
-                scale_rows(dst, whh_scales, H * half + N, N, 0, H_PASSES, X_PASSES)
-            for g in range(PASSES):
-                load_first_codes(1, g)
+            for g in range(X_PASSES + 1, X_PASSES + 4):
+                load_first_codes(0, g)
+            load_act(h_words, X_PASSES, 4, 8)
+            for g in range(X_PASSES + 4, PASSES):
+                load_first_codes(0, g)
+            for r in range(4):
+                for half in (1, 0):
+                    scale_row(plane(0, 1, half), wih_scales, H * half + N, N, 0, r)
+                    scale_row(plane(0, 1, half), whh_scales, H * half + N, N, X_PASSES, r)
+                for g in range(3 * r, 3 * r + 3):
+                    load_first_codes(1, g)
             load_block(1)
 
             turned = psum.tile([P, 2 * N], BF16, name="bank7")
@@ -227,7 +251,7 @@ def tile_koslmcell_pa_kernel(
             order = [(0, t) for t in range(T_TILES)] + [(1, t) for t in range(T_TILES)]
             for i, (half, t) in enumerate(order[:-1]):
                 acc[(half, t)] = bank(i)
-            for g in range(2):
+            for g in range(X_PASSES):
                 for half, t in order[:-1]:
                     matmul(acc[(half, t)], 0, t, half, g)
             for s in range(7):
@@ -239,10 +263,12 @@ def tile_koslmcell_pa_kernel(
             nc.vector.tensor_tensor(out=bias_cols[:], in0=bias_cols[:], in1=cols[:, 4 * P : 6 * P], op=ALU.add)
             nc.scalar.activation(out=exp_cols[:], in_=cols[:, 6 * P : 7 * P], func=ACT.Exp)
             spread_columns(0)
+            for half, t in order[:-1]:
+                matmul(acc[(half, t)], 0, t, half, X_PASSES)
             acc[(1, 3)] = bank(7)
-            for g in range(2):
+            for g in range(X_PASSES + 1):
                 matmul(acc[(1, 3)], 0, 3, 1, g)
-            for g in range(2, OUTER):
+            for g in range(X_PASSES + 1, OUTER):
                 for half, t in order:
                     matmul(acc[(half, t)], 0, t, half, g)
             load_c(1)
@@ -251,7 +277,8 @@ def tile_koslmcell_pa_kernel(
                     for g in range(OUTER, PASSES):
                         matmul(acc[(half, t)], 0, t, half, g)
                 finish_m(0, t, acc[(1, t)])
-                finish_z(0, t, acc[(0, t)])
+                start_z(0, t, acc[(0, t)])
+                end_z(0, t)
             spread_columns(1)
 
             for j in range(1, PAIRS):
@@ -265,11 +292,14 @@ def tile_koslmcell_pa_kernel(
                     for g in range(PASSES):
                         matmul(m_acc, j, t, 1, g)
                     finish_m(j, t, m_acc)
-                    edges = [0, 256, 384, 512] if last else [0, N]
-                    for i in range(len(edges) - 1):
+                    edges = [(0, 256), (256, 384), (384, 512)] if last else [(0, N)]
+                    for i, (n0, n1) in enumerate(edges):
                         z_acc = bank((t + i) % T_TILES)
                         for g in range(PASSES):
-                            matmul(z_acc, j, t, 0, g, edges[i], edges[i + 1])
-                        finish_z(j, t, z_acc, edges[i], edges[i + 1])
+                            matmul(z_acc, j, t, 0, g, n0, n1)
+                        start_z(j, t, z_acc, n0, n1)
+                        if i > 0:
+                            end_z(j, t, edges[i - 1][0], edges[i - 1][1])
+                    end_z(j, t, edges[-1][0], edges[-1][1])
                     if t == 1 and j + 1 < PAIRS:
                         spread_columns(j + 1)

@@ -43,12 +43,11 @@ def tile_koslmcell_pa_kernel(
         planes = []
         for i in range(4):
             planes.append(keep.tile([P, PASSES * 2 * N], U8, name="plane%d" % i, align_bytes=256))
-        ident = keep.tile([P, P], BF16, name="ident")
+        ident = keep.tile([P, P], F32, name="ident")
         rows = keep.tile([P, 7, 32], BF16, name="rows")
-        rows4 = keep.tile([P, 7 * P], BF16, name="rows4")
-        cols = keep.tile([P, 7 * P], F32, name="cols")
-        bias_cols = keep.tile([P, 2 * P], F32, name="bias_cols")
-        exp_cols = keep.tile([P, P], F32, name="exp_cols")
+        sums = keep.tile([P, 3, 32], F32, name="sums")
+        sums4 = keep.tile([P, 3 * P], F32, name="sums4")
+        cols = keep.tile([P, 3 * P], F32, name="cols")
 
         def plane(block, pair, half):
             if block == 0:
@@ -139,9 +138,9 @@ def tile_koslmcell_pa_kernel(
 
         def spread_columns(j):
             for key, src in (
-                ("m", bias_cols[:, P + 16 * j : P + 16 * j + 16]),
-                ("z", bias_cols[:, 16 * j : 16 * j + 16]),
-                ("e", exp_cols[:, 16 * j : 16 * j + 16]),
+                ("m", cols[:, P + 16 * j : P + 16 * j + 16]),
+                ("z", cols[:, 16 * j : 16 * j + 16]),
+                ("e", cols[:, 2 * P + 16 * j : 2 * P + 16 * j + 16]),
             ):
                 wide = work.tile([P, N], F32, name="wide", bufs=2, align_bytes=64)
                 nc.scalar.copy(
@@ -159,15 +158,17 @@ def tile_koslmcell_pa_kernel(
         prods = {}
 
         def finish_m(j, t, acc):
+            prod = work.tile([P, N], F32, name="prod", bufs=4)
+            nc.vector.tensor_tensor(out=prod[:], in0=c_tiles[j][:, t, :], in1=spread[("e", j)][:], op=ALU.mult)
             a = work.tile([P, N], F32, name="a")
             nc.vector.tensor_tensor(out=a[:], in0=acc[:], in1=spread[("m", j)][:], op=ALU.add)
             nc.scalar.activation(out=a[:], in_=a[:], func=ACT.Tanh)
             big_m = work.tile([P, N], F32, name="big_m")
             nc.scalar.mul(out=big_m[:], in_=a[:], mul=M_SCALE)
             store(j, out_m, t, 0, N, big_m[:])
-            prod = work.tile([P, N], F32, name="prod", bufs=4)
-            nc.vector.tensor_tensor(out=prod[:], in0=c_tiles[j][:, t, :], in1=spread[("e", j)][:], op=ALU.mult)
-            nc.vector.tensor_tensor(out=prod[:], in0=prod[:], in1=big_m[:], op=ALU.mult)
+            nc.vector.scalar_tensor_tensor(
+                out=prod[:], in0=a[:], scalar=M_SCALE, in1=prod[:], op0=ALU.mult, op1=ALU.mult
+            )
             prods[(j, t)] = prod
 
         zs = {}
@@ -202,7 +203,7 @@ def tile_koslmcell_pa_kernel(
             load_c(0)
 
             warm = bank(7)
-            for i in range(7):
+            for i in range(11):
                 nc.tensor.matmul(warm[:], lhsT=zeros[:, 0:P], rhs=zeros[:], start=True, stop=True)
 
             z0, m0 = plane(0, 0, 0), plane(0, 0, 1)
@@ -212,9 +213,12 @@ def tile_koslmcell_pa_kernel(
             zero(act_sc[:, X_PASSES:PASSES, :])
             zero(z0[:, X_PASSES:PASSES, :])
             zero(m0[:, X_PASSES:PASSES, :])
+            nc.vector.tensor_tensor(out=sums[:, 0:2, :], in0=rows[:, 0:2, :], in1=rows[:, 2:4, :], op=ALU.add)
+            nc.scalar.activation(out=sums[:, 2, :], in_=rows[:, 6, :], func=ACT.Exp)
+            nc.vector.tensor_tensor(out=sums[:, 0:2, :], in0=sums[:, 0:2, :], in1=rows[:, 4:6, :], op=ALU.add)
             nc.vector.tensor_copy(
-                out=rows4[:].rearrange("p (s a k) -> p s a k", s=7, a=4),
-                in_=rows[:].unsqueeze(2).to_broadcast([P, 7, 4, 32]),
+                out=sums4[:].rearrange("p (s a k) -> p s a k", s=3, a=4),
+                in_=sums[:].unsqueeze(2).to_broadcast([P, 3, 4, 32]),
             )
             zero(planes[1][:])
             zero(planes[3][:])
@@ -246,7 +250,7 @@ def tile_koslmcell_pa_kernel(
                     load_first_codes(1, g)
             load_block(1)
 
-            turned = psum.tile([P, 2 * N], BF16, name="bank7")
+            turned = bank(7)
             acc = {}
             order = [(0, t) for t in range(T_TILES)] + [(1, t) for t in range(T_TILES)]
             for i, (half, t) in enumerate(order[:-1]):
@@ -254,14 +258,9 @@ def tile_koslmcell_pa_kernel(
             for g in range(X_PASSES):
                 for half, t in order[:-1]:
                     matmul(acc[(half, t)], 0, t, half, g)
-            for s in range(7):
-                nc.tensor.transpose(turned[:, P * s : P * (s + 1)], rows4[:, P * s : P * (s + 1)], ident[:])
-            nc.scalar.copy(out=cols[:], in_=turned[:, 0 : 7 * P])
-            nc.vector.tensor_tensor(
-                out=bias_cols[:], in0=cols[:, 0 : 2 * P], in1=cols[:, 2 * P : 4 * P], op=ALU.add
-            )
-            nc.vector.tensor_tensor(out=bias_cols[:], in0=bias_cols[:], in1=cols[:, 4 * P : 6 * P], op=ALU.add)
-            nc.scalar.activation(out=exp_cols[:], in_=cols[:, 6 * P : 7 * P], func=ACT.Exp)
+            for s in range(3):
+                nc.tensor.transpose(turned[:, P * s : P * (s + 1)], sums4[:, P * s : P * (s + 1)], ident[:])
+            nc.scalar.copy(out=cols[:], in_=turned[:, 0 : 3 * P])
             spread_columns(0)
             for half, t in order[:-1]:
                 matmul(acc[(half, t)], 0, t, half, X_PASSES)
@@ -286,12 +285,14 @@ def tile_koslmcell_pa_kernel(
                     load_block(j // 2 + 1)
                 if j + 1 < PAIRS:
                     load_c(j + 1)
+                early = j == PAIRS - 1
                 for t in range(T_TILES):
-                    last = j == PAIRS - 1 and t == T_TILES - 1
-                    m_acc = bank(4 + t)
-                    for g in range(PASSES):
-                        matmul(m_acc, j, t, 1, g)
-                    finish_m(j, t, m_acc)
+                    last = early and t == T_TILES - 1
+                    for tm in ((t,) if not early or t < 2 else (2, 3) if t == 2 else ()):
+                        m_acc = bank(4 + tm)
+                        for g in range(PASSES):
+                            matmul(m_acc, j, tm, 1, g)
+                        finish_m(j, tm, m_acc)
                     edges = [(0, 256), (256, 384), (384, 512)] if last else [(0, N)]
                     for i, (n0, n1) in enumerate(edges):
                         z_acc = bank((t + i) % T_TILES)

from contextlib import ExitStack

import concourse.mybir as mybir
from concourse.masks import make_identity

F32 = mybir.dt.float32
BF16 = mybir.dt.bfloat16
I32 = mybir.dt.int32
U8 = mybir.dt.uint8
FP4X4 = mybir.dt.float4_e2m1fn_x4
ACT = mybir.ActivationFunctionType
ALU = mybir.AluOpType

B, D, H = 512, 2048, 4096
M_SCALE = 1.5
FLOPS = 2 * B * (D + H) * 2 * H

P = 128
X_PASSES = D // 512
H_PASSES = H // 512
PASSES = X_PASSES + H_PASSES
T_TILES = B // P
N = 512
PAIRS = H // N
BLOCKS = PAIRS // 2
OUTER = 8


def tile_koslmcell_pa_kernel(
    tc, x_words, x_scales, h_words, h_scales, c_prev, wih_words, wih_scales, b_ih,
    whh_words, whh_scales, b_hh, log_lambda, z_bias, m_bias, out_z, out_m, out_innov,
):
    nc = tc.nc

    with ExitStack() as ctx:
        keep = ctx.enter_context(tc.tile_pool(name="keep", bufs=1))
        wpool = ctx.enter_context(tc.tile_pool(name="wpool", bufs=4 * PASSES))
        work = ctx.enter_context(tc.tile_pool(name="work", bufs=3))
        psum = ctx.enter_context(tc.psum_pool(name="psum", bufs=1))

        act = keep.tile([P, PASSES, 2 * B], U8, name="act", align_bytes=256)
        act_sc = keep.tile([P, PASSES, B], U8, name="act_sc", align_bytes=256)
        planes = []
        for i in range(4):
            planes.append(keep.tile([P, PASSES * 2 * N], U8, name="plane%d" % i, align_bytes=256))
        ident = keep.tile([P, P], F32, name="ident")
        rows = keep.tile([P, 7, 32], BF16, name="rows")
        sums = keep.tile([P, 3, 32], F32, name="sums")
        sums4 = keep.tile([P, 3 * P], F32, name="sums4")
        cols = keep.tile([P, 3 * P], F32, name="cols")

        def plane(block, pair, half):
            if block == 0:
                region = planes[pair][:, half * PASSES * N : (half + 1) * PASSES * N]
                return region.rearrange("p (g n) -> p g n", n=N)
            whole = planes[2 * (block % 2) + half][:].rearrange("p (g n) -> p g n", n=2 * N)
            return whole[:, :, pair * N : (pair + 1) * N]

        def scale_rows(dst, src, c0, width, g0, g1, first):
            for quad in (0, 2, 1, 3):
                nc.sync.dma_start(
                    out=dst[32 * quad : 32 * quad + 4, g0 + first : g1 + first, :].bitcast(I32),
                    in_=src[g0:g1, 4 * quad : 4 * quad + 4, c0 : c0 + width].rearrange("g q n -> q g n").bitcast(I32),
                )

        def scale_row(dst, src, c0, width, first, r):
            nc.sync.dma_start(
                out=dst[r:P:32, first : first + src.shape[0], :].bitcast(I32),
                in_=src[:, r:16:4, c0 : c0 + width].rearrange("g q n -> q g n").bitcast(I32),
            )

        def load_act(src, first, g0, g1):
            nc.sync.dma_start(
                out=act[:, first + g0 : first + g1, :].bitcast(I32),
                in_=src[g0:g1].rearrange("g p n -> p g n").bitcast(I32),
            )

        def words_of(g):
            return wih_words[g] if g < X_PASSES else whh_words[g - X_PASSES]

        w_tiles = {}

        def load_first_codes(pair, g):
            w = wpool.tile([P, 4 * N], U8, name="w", align_bytes=256)
            src = words_of(g).rearrange("p (h n) -> p h n", h=2)[:, :, 2 * N * pair : 2 * N * (pair + 1)]
            nc.sync.dma_start(
                out=w[:].rearrange("p (h n) -> p h n", h=2).bitcast(I32),
                in_=src.bitcast(I32),
            )
            w_tiles[(0, pair, g)] = w

        def load_codes(block, half, g):
            w = wpool.tile([P, 4 * N], U8, name="w", align_bytes=256)
            c0 = 2 * H * half + 4 * N * block
            nc.sync.dma_start(out=w[:].bitcast(I32), in_=words_of(g)[:, c0 : c0 + 4 * N].bitcast(I32))
            w_tiles[(block, half, g)] = w

        def load_block(block):
            for r in range(4):
                for half in (1, 0):
                    dst = planes[2 * (block % 2) + half][:].rearrange("p (g n) -> p g n", n=2 * N)
                    c0 = H * half + 2 * N * block
                    scale_row(dst, wih_scales, c0, 2 * N, 0, r)
                    scale_row(dst, whh_scales, c0, 2 * N, X_PASSES, r)
                for half in (1, 0):
                    for g in range(3 * r, 3 * r + 3):
                        load_codes(block, half, g)

        def codes(block, pair, half, g):
            if block == 0:
                return w_tiles[(0, pair, g)][:, 2 * N * half : 2 * N * (half + 1)]
            return w_tiles[(block, half, g)][:, 2 * N * pair : 2 * N * (pair + 1)]

        def matmul(acc, j, t, half, g, n0=0, n1=N):
            block, pair = j // 2, j % 2
            nc.tensor.matmul_mx(
                out=acc[:, 0 : n1 - n0],
                lhsT=act[:, g, 2 * P * t : 2 * P * (t + 1)].bitcast(FP4X4),
                lhsT_scale=act_sc[:, g, P * t : P * (t + 1)],
                rhs=codes(block, pair, half, g)[:, 2 * n0 : 2 * n1].bitcast(FP4X4),
                rhs_scale=plane(block, pair, half)[:, g, n0:n1],
                start=(g == 0),
                stop=(g == PASSES - 1),
            )

        def bank(i):
            return psum.tile([P, N], F32, name="bank%d" % i)

        c_view = c_prev.rearrange("(t p) n -> p t n", p=P)
        c_tiles = {}

        def load_c(j):
            c = work.tile([P, T_TILES, N], BF16, name="c", bufs=2)
            nc.gpsimd.dma_start(out=c[:], in_=c_view[:, :, j * N : (j + 1) * N])
            c_tiles[j] = c

        spread = {}

        def spread_columns(j):
            for key, src in (
                ("m", cols[:, P + 16 * j : P + 16 * j + 16]),
                ("z", cols[:, 16 * j : 16 * j + 16]),
                ("e", cols[:, 2 * P + 16 * j : 2 * P + 16 * j + 16]),
            ):
                wide = work.tile([P, N], F32, name="wide", bufs=2, align_bytes=64)
                nc.scalar.copy(
                    out=wide[:].rearrange("p (b i) -> p b i", i=32),
                    in_=src.unsqueeze(2).to_broadcast([P, 16, 32]),
                )
                full = work.tile([P, N], F32, name="full_" + key, bufs=2, align_bytes=64)
                nc.vector.transpose(full[:], wide[:])
                spread[(key, j)] = full

        def store(j, out, t, n0, n1, tile):
            eng = nc.sync if j >= PAIRS - 2 else nc.gpsimd
            eng.dma_start(out=out[P * t : P * (t + 1), j * N + n0 : j * N + n1], in_=tile)

        prods = {}

        def finish_m(j, t, acc):
            prod = work.tile([P, N], F32, name="prod", bufs=4)
            nc.vector.tensor_tensor(out=prod[:], in0=c_tiles[j][:, t, :], in1=spread[("e", j)][:], op=ALU.mult)
            a = work.tile([P, N], F32, name="a")
            nc.vector.tensor_tensor(out=a[:], in0=acc[:], in1=spread[("m", j)][:], op=ALU.add)
            nc.scalar.activation(out=a[:], in_=a[:], func=ACT.Tanh)
            big_m = work.tile([P, N], F32, name="big_m")
            nc.scalar.mul(out=big_m[:], in_=a[:], mul=M_SCALE)
            store(j, out_m, t, 0, N, big_m[:])
            nc.vector.scalar_tensor_tensor(
                out=prod[:], in0=a[:], scalar=M_SCALE, in1=prod[:], op0=ALU.mult, op1=ALU.mult
            )
            prods[(j, t)] = prod

        zs = {}

        def start_z(j, t, acc, n0=0, n1=N):
            w = n1 - n0
            z = work.tile([P, N], F32, name="z")
            nc.vector.tensor_tensor(out=z[:, 0:w], in0=acc[:, 0:w], in1=spread[("z", j)][:, n0:n1], op=ALU.add)
            nc.scalar.activation(out=z[:, 0:w], in_=z[:, 0:w], func=ACT.Tanh)
            store(j, out_z, t, n0, n1, z[:, 0:w])
            zs[(j, t, n0)] = z

        def end_z(j, t, n0=0, n1=N):
            w = n1 - n0
            z = zs[(j, t, n0)]
            innov = prods[(j, t)][:, n0:n1]
            nc.vector.tensor_tensor(out=innov, in0=innov, in1=z[:, 0:w], op=ALU.add)
            store(j, out_innov, t, n0, n1, innov)

        def zero(view):
            nc.vector.memset(view.bitcast(I32), 0)

        with tc.manual_schedule():
            zeros = keep.tile([P, N], BF16, name="zeros")
            nc.gpsimd.memset(zeros[:], 0.0)
            nc.gpsimd.dma_start(out=rows[:, 0:2, :], in_=b_ih.rearrange("(s b k) -> b s k", s=2, k=32))
            nc.gpsimd.dma_start(out=rows[:, 2:4, :], in_=b_hh.rearrange("(s b k) -> b s k", s=2, k=32))
            nc.gpsimd.dma_start(out=rows[:, 4, :], in_=z_bias.rearrange("(b k) -> b k", k=32))
            nc.gpsimd.dma_start(out=rows[:, 5, :], in_=m_bias.rearrange("(b k) -> b k", k=32))
            nc.gpsimd.dma_start(out=rows[:, 6, :], in_=log_lambda.rearrange("(b k) -> b k", k=32))
            make_identity(nc, ident[:])
            load_c(0)

            warm = bank(7)
            for i in range(11):
                nc.tensor.matmul(warm[:], lhsT=zeros[:, 0:P], rhs=zeros[:], start=True, stop=True)

            z0, m0 = plane(0, 0, 0), plane(0, 0, 1)
            zero(act_sc[:, 0:X_PASSES, :])
            zero(z0[:, 0:X_PASSES, :])
            zero(m0[:, 0:X_PASSES, :])
            zero(act_sc[:, X_PASSES:PASSES, :])
            zero(z0[:, X_PASSES:PASSES, :])
            zero(m0[:, X_PASSES:PASSES, :])
            nc.vector.tensor_tensor(out=sums[:, 0:2, :], in0=rows[:, 0:2, :], in1=rows[:, 2:4, :], op=ALU.add)
            nc.scalar.activation(out=sums[:, 2, :], in_=rows[:, 6, :], func=ACT.Exp)
            nc.vector.tensor_tensor(out=sums[:, 0:2, :], in0=sums[:, 0:2, :], in1=rows[:, 4:6, :], op=ALU.add)
            nc.vector.tensor_copy(
                out=sums4[:].rearrange("p (s a k) -> p s a k", s=3, a=4),
                in_=sums[:].unsqueeze(2).to_broadcast([P, 3, 4, 32]),
            )
            zero(planes[1][:])
            zero(planes[3][:])
            zero(planes[2][:])

            load_act(x_words, 0, 0, 1)
            load_first_codes(0, 0)
            scale_rows(act_sc, x_scales, 0, B, 0, X_PASSES, 0)
            scale_rows(z0, wih_scales, 0, N, 0, X_PASSES, 0)
            scale_rows(m0, wih_scales, H, N, 0, X_PASSES, 0)
            load_act(x_words, 0, 1, 4)
            for g in range(1, X_PASSES):
                load_first_codes(0, g)
            scale_rows(act_sc, h_scales, 0, B, 0, H_PASSES, X_PASSES)
            scale_rows(z0, whh_scales, 0, N, 0, H_PASSES, X_PASSES)
            load_act(h_words, X_PASSES, 0, 4)
            load_first_codes(0, X_PASSES)
            scale_rows(m0, whh_scales, H, N, 0, H_PASSES, X_PASSES)
            for g in range(X_PASSES + 1, X_PASSES + 4):
                load_first_codes(0, g)
            load_act(h_words, X_PASSES, 4, 8)
            for g in range(X_PASSES + 4, PASSES):
                load_first_codes(0, g)
            for r in range(4):
                for half in (1, 0):
                    scale_row(plane(0, 1, half), wih_scales, H * half + N, N, 0, r)
                    scale_row(plane(0, 1, half), whh_scales, H * half + N, N, X_PASSES, r)
                for g in range(3 * r, 3 * r + 3):
                    load_first_codes(1, g)
            load_block(1)

            turned = bank(7)
            acc = {}
            order = [(0, t) for t in range(T_TILES)] + [(1, t) for t in range(T_TILES)]
            for i, (half, t) in enumerate(order[:-1]):
                acc[(half, t)] = bank(i)
            for g in range(X_PASSES):
                for half, t in order[:-1]:
                    matmul(acc[(half, t)], 0, t, half, g)
            for s in range(3):
                nc.tensor.transpose(turned[:, P * s : P * (s + 1)], sums4[:, P * s : P * (s + 1)], ident[:])
            nc.scalar.copy(out=cols[:], in_=turned[:, 0 : 3 * P])
            spread_columns(0)
            for half, t in order[:-1]:
                matmul(acc[(half, t)], 0, t, half, X_PASSES)
            acc[(1, 3)] = bank(7)
            for g in range(X_PASSES + 1):
                matmul(acc[(1, 3)], 0, 3, 1, g)
            for g in range(X_PASSES + 1, OUTER):
                for half, t in order:
                    matmul(acc[(half, t)], 0, t, half, g)
            load_c(1)
            for t in range(T_TILES):
                for half in (1, 0):
                    for g in range(OUTER, PASSES):
                        matmul(acc[(half, t)], 0, t, half, g)
                finish_m(0, t, acc[(1, t)])
                start_z(0, t, acc[(0, t)])
                end_z(0, t)
            spread_columns(1)

            for j in range(1, PAIRS):
                if j % 2 == 0 and j // 2 + 1 < BLOCKS:
                    load_block(j // 2 + 1)
                if j + 1 < PAIRS:
                    load_c(j + 1)
                early = j == PAIRS - 1
                for t in range(T_TILES):
                    last = early and t == T_TILES - 1
                    for tm in ((t,) if not early or t < 2 else (2, 3) if t == 2 else ()):
                        m_acc = bank(4 + tm)
                        for g in range(PASSES):
                            matmul(m_acc, j, tm, 1, g)
                        finish_m(j, tm, m_acc)
                    edges = [(0, 256), (256, 384), (384, 512)] if last else [(0, N)]
                    for i, (n0, n1) in enumerate(edges):
                        z_acc = bank((t + i) % T_TILES)
                        for g in range(PASSES):
                            matmul(z_acc, j, t, 0, g, n0, n1)
                        start_z(j, t, z_acc, n0, n1)
                        if i > 0:
                            end_z(j, t, edges[i - 1][0], edges[i - 1][1])
                    end_z(j, t, edges[-1][0], edges[-1][1])
                    if t == 1 and j + 1 < PAIRS:
                        spread_columns(j + 1)
